import numpy as np
import ml_dtypes


def mxq(x, axis, fmt="e4m3"):
    dtype, down = {"e4m3": (ml_dtypes.float8_e4m3fn, 7), "e5m2": (ml_dtypes.float8_e5m2, 14)}[fmt]
    v = np.moveaxis(np.asarray(x, np.float32).astype(ml_dtypes.bfloat16).astype(np.float64), axis, -1)
    blocks = v.reshape(v.shape[:-1] + (-1, 32))
    amax = np.abs(blocks).max(-1, keepdims=True)
    byte = np.maximum(np.where(amax > 0, np.frexp(amax)[1] - 1 + 127, 0) - down, 1)
    scale = np.exp2(byte - 127.0)
    codes = (blocks / scale).astype(np.float32).astype(dtype).astype(np.float64)
    return np.moveaxis((codes * scale).reshape(v.shape), -1, axis)


WIDE = False


def mx_kscale(k):
    if not WIDE:
        return np.ones(k)
    levels = np.array([10, -10, 5, -5, 0])
    a = np.random.permutation(np.resize(levels, k // 512 * 4)).reshape(k // 512, 4)
    idx = np.arange(k)
    return np.exp2(a[idx // 512, idx % 128 // 32])


BF16 = ml_dtypes.bfloat16


def bf(x):
    return np.asarray(x, np.float32).astype(BF16)


def f64(x):
    return np.asarray(x).astype(np.float64)


B, F, H, E = 256, 128, 512, 128


def setup_inputs():
    t = mx_kscale(H)
    return {"x": bf(np.random.standard_normal((B, F))),
            "w1": bf(np.random.uniform(-1.0, 1.0, (F, H)) * t),
            "b1": bf(np.random.uniform(-1.0, 1.0, (F, H)) * t),
            "w2": bf(np.random.standard_normal((F, H, E)) * 1.5 / np.sqrt(H) / t[None, :, None]),
            "b2": bf(np.random.standard_normal((F, E)) * 0.3)}


def reference(x, w1, b1, w2, b2):
    h = np.maximum(f64(x)[:, :, None] * f64(w1)[None] + f64(b1)[None], 0.0)
    hq = mxq(h, 2, "e4m3")
    out = (hq.transpose(1, 0, 2) @ mxq(f64(w2), 1, "e4m3")).transpose(1, 0, 2) + f64(b2)[None]
    return out.reshape(x.shape[0], F * E)

@@ -1,0 +1,208 @@
+from contextlib import ExitStack
+
+import concourse.mybir as mybir
+from concourse.masks import make_identity
+
+FLOPS = 2 * 256 * 128 * 512 * 128
+
+BF16 = mybir.dt.bfloat16
+F32 = mybir.dt.float32
+U32 = mybir.dt.uint32
+U8 = mybir.dt.uint8
+FP8X4 = mybir.dt.float8_e4m3fn_x4
+ALU = mybir.AluOpType
+ACT = mybir.ActivationFunctionType
+
+P = 128
+PACK = 4
+B, F, H, E = 256, 128, 512, 128
+NBC = B // P
+GF = 4
+NG = F // GF
+WF = 8
+OG = 4
+
+
+def tile_densefeaturenumericembedding_kernel(tc, x, w1, b1, w2, b2, out):
+    nc = tc.nc
+    with ExitStack() as ctx:
+        const = ctx.enter_context(tc.tile_pool(name="const", bufs=1))
+        wraw_pool = ctx.enter_context(tc.tile_pool(name="wraw", bufs=3))
+        wq_pool = ctx.enter_context(tc.tile_pool(name="wq", bufs=3))
+        h_pool = ctx.enter_context(tc.tile_pool(name="h", bufs=3))
+        o_pool = ctx.enter_context(tc.tile_pool(name="o", bufs=3))
+        ps_x = ctx.enter_context(tc.psum_pool(name="psx", bufs=2))
+        ps_o = ctx.enter_context(tc.psum_pool(name="pso", bufs=6))
+
+        x_sb = const.tile([P, NBC, F], BF16)
+        nc.sync.dma_start(out=x_sb[:], in_=x.rearrange("(c p) f -> p c f", p=P))
+        w1_sb = const.tile([P, H], BF16)
+        nc.sync.dma_start(out=w1_sb[:], in_=w1)
+        b1_sb = const.tile([P, H], BF16)
+        nc.sync.dma_start(out=b1_sb[:], in_=b1)
+
+        ident_bf = const.tile([P, P], BF16)
+        make_identity(nc, ident_bf[:])
+        ident_f = const.tile([P, P], F32)
+        make_identity(nc, ident_f[:])
+
+        wraw = {}
+
+        def load_w(ch):
+            t = wraw_pool.tile([P, WF, PACK * E], BF16, name="w2raw")
+            nc.sync.dma_start(
+                out=t[:],
+                in_=w2[ch * WF : (ch + 1) * WF].rearrange("f (p j) e -> p f (j e)", j=PACK),
+            )
+            wraw[ch] = t
+
+        load_w(0)
+
+        b2bc = const.tile([P, F * E], BF16)
+        b2flat = b2.rearrange("f e -> (f e)")
+        NB2 = 4
+        for i in range(NB2):
+            n = F * E // NB2
+            nc.sync.dma_start(
+                out=b2bc[:, i * n : (i + 1) * n],
+                in_=b2flat[i * n : (i + 1) * n].partition_broadcast(P),
+            )
+
+        scal = []
+        for src in (w1_sb, b1_sb):
+            r = const.tile([P, PACK, P], F32, name="wr32", tag="wr32_%d" % len(scal))
+            nc.vector.tensor_copy(out=r[:], in_=src[:].rearrange("f (p t) -> f t p", t=PACK))
+            ps = ps_o.tile([P, PACK, P], F32, name="po", tag="po")
+            for t in range(PACK):
+                nc.tensor.transpose(ps[:, t, :], r[:, t, :], ident_f[:])
+            s = const.tile([P, PACK, F], F32, name="scalT", tag="scalT_%d" % len(scal))
+            nc.vector.tensor_copy(out=s[:], in_=ps[:])
+            scal.append(s)
+        w1T, b1T = scal
+
+        xb, at, gt, hq, wq, ops, ot = {}, {}, {}, {}, {}, {}, {}
+
+        def stage_x(g):
+            ps = ps_x.tile([P, GF, B], BF16, name="xps")
+            for fi in range(GF):
+                f = g * GF + fi
+                for c in range(NBC):
+                    nc.tensor.transpose(
+                        ps[:, fi, c * P : (c + 1) * P],
+                        x_sb[:, c, f : f + 1].to_broadcast([P, P]),
+                        ident_bf[:],
+                    )
+            t = h_pool.tile([P, GF, B], BF16, name="xb")
+            nc.scalar.copy(out=t[:], in_=ps[:])
+            xb[g] = t
+
+        def stage_a(g):
+            a = h_pool.tile([P, PACK, GF, B], BF16, name="a")
+            for t in range(PACK):
+                for fi in range(GF):
+                    f = g * GF + fi
+                    nc.vector.tensor_scalar(
+                        out=a[:, t, fi, :],
+                        in0=xb[g][:, fi, :],
+                        scalar1=w1T[:, t, f : f + 1],
+                        scalar2=b1T[:, t, f : f + 1],
+                        op0=ALU.mult,
+                        op1=ALU.add,
+                    )
+            at[g] = a
+
+        def stage_b(g):
+            gr = h_pool.tile([P, GF * B, PACK], BF16, name="gr", align_bytes=64)
+            nc.scalar.activation(
+                out=gr[:].rearrange("p (c i) t -> p c t i", i=4),
+                in_=at[g][:].rearrange("p t f b -> p t (f b)").rearrange("p t (c i) -> p c t i", i=4),
+                func=ACT.Relu,
+            )
+            gt[g] = gr
+
+        def stage_q(g):
+            hc = h_pool.tile([P, GF * B], U32, name="hc", align_bytes=64)
+            hs = h_pool.tile([P, GF * B], U8, name="hs", align_bytes=64)
+            nc.vector.quantize_mx(
+                out=hc[:].bitcast(FP8X4),
+                scales=hs[:],
+                in_=gt[g][:].rearrange("p c t -> p (c t)"),
+            )
+            hq[g] = (hc, hs)
+
+        def stage_w(g):
+            ch, off = divmod(g * GF, WF)
+            if off == 0 and ch + 1 < F // WF:
+                load_w(ch + 1)
+            wg = wq_pool.tile([P, GF, E, PACK], BF16, name="wg", align_bytes=64)
+            nc.vector.tensor_copy(
+                out=wg[:].rearrange("p f (c i) t -> p f c t i", i=4),
+                in_=wraw[ch][:, off : off + GF, :].rearrange("p f (t c i) -> p f c t i", t=PACK, i=4),
+            )
+            wc = wq_pool.tile([P, GF * E], U32, name="wc", align_bytes=64)
+            ws = wq_pool.tile([P, GF * E], U8, name="ws", align_bytes=64)
+            nc.vector.quantize_mx(
+                out=wc[:].bitcast(FP8X4),
+                scales=ws[:],
+                in_=wg[:].rearrange("p f e t -> p (f e t)"),
+            )
+            wq[g] = (wc, ws)
+
+        def stage_mm(g):
+            hc, hs = hq[g]
+            wc, ws = wq[g]
+            tiles = []
+            for c in range(NBC):
+                po = ps_o.tile([P, GF * E], F32, name="po", tag="po")
+                for fi in range(GF):
+                    hcol = slice(fi * B + c * P, fi * B + (c + 1) * P)
+                    wcol = slice(fi * E, (fi + 1) * E)
+                    nc.tensor.matmul_mx(
+                        out=po[:, wcol],
+                        lhsT=hc[:, hcol].bitcast(FP8X4),
+                        lhsT_scale=hs[:, hcol],
+                        rhs=wc[:, wcol].bitcast(FP8X4),
+                        rhs_scale=ws[:, wcol],
+                        start=True,
+                        stop=True,
+                    )
+                tiles.append(po)
+            ops[g] = tiles
+
+        def stage_o(g):
+            og, pos = divmod(g, OG)
+            if pos == 0:
+                ot[og] = o_pool.tile([P, NBC, OG * GF * E], F32, name="ot")
+            o = ot[og]
+            w = GF * E
+            for c in range(NBC):
+                nc.vector.tensor_tensor(
+                    out=o[:, c, pos * w : (pos + 1) * w],
+                    in0=ops[g][c][:],
+                    in1=b2bc[:, g * w : (g + 1) * w],
+                    op=ALU.add,
+                )
+            if pos == OG - 1:
+                for c in range(NBC):
+                    nc.sync.dma_start(
+                        out=out[c * P : (c + 1) * P, og * OG * w : (og + 1) * OG * w],
+                        in_=o[:, c, :],
+                    )
+
+        stage_x(0)
+        stage_x(1)
+        stage_a(0)
+        stage_b(0)
+        stage_a(1)
+        for i in range(NG):
+            if i + 2 < NG:
+                stage_x(i + 2)
+                stage_a(i + 2)
+            if i + 1 < NG:
+                stage_b(i + 1)
+            stage_w(i)
+            stage_q(i)
+            stage_mm(i)
+            if i >= 1:
+                stage_o(i - 1)
+        stage_o(NG - 1)

@@ -20,31 +20,25 @@ NBC = B // P
 GF = 4
 NG = F // GF
 WF = 8
-OG = 4
+NCH = F // WF
+GW = GF * E
+S_EVERY = 4
+STORES = [4, 4, 4, 4, 4, 4, 4, 2, 1, 1]
+NB2 = 4
 
 
 def tile_densefeaturenumericembedding_kernel(tc, x, w1, b1, w2, b2, out):
     nc = tc.nc
     with ExitStack() as ctx:
         const = ctx.enter_context(tc.tile_pool(name="const", bufs=1))
-        wraw_pool = ctx.enter_context(tc.tile_pool(name="wraw", bufs=3))
+        wraw_pool = ctx.enter_context(tc.tile_pool(name="wraw", bufs=4))
+        wg_pool = ctx.enter_context(tc.tile_pool(name="wg", bufs=4))
         wq_pool = ctx.enter_context(tc.tile_pool(name="wq", bufs=3))
         h_pool = ctx.enter_context(tc.tile_pool(name="h", bufs=3))
-        o_pool = ctx.enter_context(tc.tile_pool(name="o", bufs=3))
+        o_pool = ctx.enter_context(tc.tile_pool(name="o", bufs=2))
         ps_x = ctx.enter_context(tc.psum_pool(name="psx", bufs=2))
         ps_o = ctx.enter_context(tc.psum_pool(name="pso", bufs=6))
-
-        x_sb = const.tile([P, NBC, F], BF16)
-        nc.sync.dma_start(out=x_sb[:], in_=x.rearrange("(c p) f -> p c f", p=P))
-        w1_sb = const.tile([P, H], BF16)
-        nc.sync.dma_start(out=w1_sb[:], in_=w1)
-        b1_sb = const.tile([P, H], BF16)
-        nc.sync.dma_start(out=b1_sb[:], in_=b1)
-
-        ident_bf = const.tile([P, P], BF16)
-        make_identity(nc, ident_bf[:])
-        ident_f = const.tile([P, P], F32)
-        make_identity(nc, ident_f[:])
+        ctx.enter_context(tc.manual_schedule())
 
         wraw = {}
 
@@ -56,31 +50,37 @@ def tile_densefeaturenumericembedding_kernel(tc, x, w1, b1, w2, b2, out):
             )
             wraw[ch] = t
 
-        load_w(0)
-
         b2bc = const.tile([P, F * E], BF16)
         b2flat = b2.rearrange("f e -> (f e)")
-        NB2 = 4
-        for i in range(NB2):
+
+        def load_b2(i):
             n = F * E // NB2
             nc.sync.dma_start(
                 out=b2bc[:, i * n : (i + 1) * n],
                 in_=b2flat[i * n : (i + 1) * n].partition_broadcast(P),
             )
 
-        scal = []
-        for src in (w1_sb, b1_sb):
-            r = const.tile([P, PACK, P], F32, name="wr32", tag="wr32_%d" % len(scal))
-            nc.vector.tensor_copy(out=r[:], in_=src[:].rearrange("f (p t) -> f t p", t=PACK))
-            ps = ps_o.tile([P, PACK, P], F32, name="po", tag="po")
-            for t in range(PACK):
-                nc.tensor.transpose(ps[:, t, :], r[:, t, :], ident_f[:])
-            s = const.tile([P, PACK, F], F32, name="scalT", tag="scalT_%d" % len(scal))
-            nc.vector.tensor_copy(out=s[:], in_=ps[:])
-            scal.append(s)
-        w1T, b1T = scal
+        x_sb = const.tile([P, NBC, F], BF16)
+        nc.sync.dma_start(out=x_sb[:], in_=x.rearrange("(c p) f -> p c f", p=P))
+        w1_sb = const.tile([P, H], BF16)
+        nc.sync.dma_start(out=w1_sb[:], in_=w1)
+        b1_sb = const.tile([P, H], BF16)
+        nc.sync.dma_start(out=b1_sb[:], in_=b1)
+        load_w(0)
+        load_w(1)
+        load_b2(0)
+        load_w(2)
+        load_b2(1)
+        load_w(3)
+        load_b2(2)
+        load_b2(3)
 
-        xb, at, gt, hq, wq, ops, ot = {}, {}, {}, {}, {}, {}, {}
+        ident_bf = const.tile([P, P], BF16)
+        make_identity(nc, ident_bf[:])
+        ident_f = const.tile([P, P], F32)
+        make_identity(nc, ident_f[:])
+
+        xb, at, gt, hq, wgt, wq, ops, ot = {}, {}, {}, {}, {}, {}, {}, {}
 
         def stage_x(g):
             ps = ps_x.tile([P, GF, B], BF16, name="xps")
@@ -95,6 +95,20 @@ def tile_densefeaturenumericembedding_kernel(tc, x, w1, b1, w2, b2, out):
             t = h_pool.tile([P, GF, B], BF16, name="xb")
             nc.scalar.copy(out=t[:], in_=ps[:])
             xb[g] = t
+
+        stage_x(0)
+
+        scal = []
+        for src in (w1_sb, b1_sb):
+            r = const.tile([P, PACK, P], F32, name="wr32", tag="wr32_%d" % len(scal))
+            nc.vector.tensor_copy(out=r[:], in_=src[:].rearrange("f (p t) -> f t p", t=PACK))
+            ps = ps_o.tile([P, PACK, P], F32, name="po", tag="po")
+            for t in range(PACK):
+                nc.tensor.transpose(ps[:, t, :], r[:, t, :], ident_f[:])
+            s = const.tile([P, PACK, F], F32, name="scalT", tag="scalT_%d" % len(scal))
+            nc.vector.tensor_copy(out=s[:], in_=ps[:])
+            scal.append(s)
+        w1T, b1T = scal
 
         def stage_a(g):
             a = h_pool.tile([P, PACK, GF, B], BF16, name="a")
@@ -130,21 +144,32 @@ def tile_densefeaturenumericembedding_kernel(tc, x, w1, b1, w2, b2, out):
             )
             hq[g] = (hc, hs)
 
-        def stage_w(g):
+        def on_scalar(g):
+            return g % S_EVERY == 0
+
+        def stage_wr(g):
             ch, off = divmod(g * GF, WF)
-            if off == 0 and ch + 1 < F // WF:
-                load_w(ch + 1)
-            wg = wq_pool.tile([P, GF, E, PACK], BF16, name="wg", align_bytes=64)
-            nc.vector.tensor_copy(
-                out=wg[:].rearrange("p f (c i) t -> p f c t i", i=4),
-                in_=wraw[ch][:, off : off + GF, :].rearrange("p f (t c i) -> p f c t i", t=PACK, i=4),
-            )
-            wc = wq_pool.tile([P, GF * E], U32, name="wc", align_bytes=64)
-            ws = wq_pool.tile([P, GF * E], U8, name="ws", align_bytes=64)
+            wg = wg_pool.tile([P, GF, E, PACK], BF16, name="wg", align_bytes=64)
+            if on_scalar(g):
+                for fi in range(GF):
+                    nc.scalar.copy(
+                        out=wg[:, fi].rearrange("p (c i) t -> p c t i", i=4),
+                        in_=wraw[ch][:, off + fi, :].rearrange("p (t c i) -> p c t i", t=PACK, i=4),
+                    )
+            else:
+                nc.vector.tensor_copy(
+                    out=wg[:].rearrange("p f (c i) t -> p f c t i", i=4),
+                    in_=wraw[ch][:, off : off + GF, :].rearrange("p f (t c i) -> p f c t i", t=PACK, i=4),
+                )
+            wgt[g] = wg
+
+        def stage_wq(g):
+            wc = wq_pool.tile([P, GW], U32, name="wc", align_bytes=64)
+            ws = wq_pool.tile([P, GW], U8, name="ws", align_bytes=64)
             nc.vector.quantize_mx(
                 out=wc[:].bitcast(FP8X4),
                 scales=ws[:],
-                in_=wg[:].rearrange("p f e t -> p (f e t)"),
+                in_=wgt[g][:].rearrange("p f e t -> p (f e t)"),
             )
             wq[g] = (wc, ws)
 
@@ -153,7 +178,7 @@ def tile_densefeaturenumericembedding_kernel(tc, x, w1, b1, w2, b2, out):
             wc, ws = wq[g]
             tiles = []
             for c in range(NBC):
-                po = ps_o.tile([P, GF * E], F32, name="po", tag="po")
+                po = ps_o.tile([P, GW], F32, name="po", tag="po")
                 for fi in range(GF):
                     hcol = slice(fi * B + c * P, fi * B + (c + 1) * P)
                     wcol = slice(fi * E, (fi + 1) * E)
@@ -169,40 +194,56 @@ def tile_densefeaturenumericembedding_kernel(tc, x, w1, b1, w2, b2, out):
                 tiles.append(po)
             ops[g] = tiles
 
+        first_of = {}
+        last_of = {}
+        g0 = 0
+        for n in STORES:
+            for g in range(g0, g0 + n):
+                first_of[g] = g0
+                last_of[g] = g0 + n - 1
+            g0 += n
+        assert g0 == NG
+
         def stage_o(g):
-            og, pos = divmod(g, OG)
-            if pos == 0:
-                ot[og] = o_pool.tile([P, NBC, OG * GF * E], F32, name="ot")
-            o = ot[og]
-            w = GF * E
+            lo, hi = first_of[g], last_of[g]
+            if g == lo:
+                ot[lo] = o_pool.tile([P, NBC, max(STORES) * GW], F32, name="ot")
+            o = ot[lo]
+            pos = g - lo
             for c in range(NBC):
                 nc.vector.tensor_tensor(
-                    out=o[:, c, pos * w : (pos + 1) * w],
+                    out=o[:, c, pos * GW : (pos + 1) * GW],
                     in0=ops[g][c][:],
-                    in1=b2bc[:, g * w : (g + 1) * w],
+                    in1=b2bc[:, g * GW : (g + 1) * GW],
                     op=ALU.add,
                 )
-            if pos == OG - 1:
+            if g == hi:
                 for c in range(NBC):
                     nc.sync.dma_start(
-                        out=out[c * P : (c + 1) * P, og * OG * w : (og + 1) * OG * w],
-                        in_=o[:, c, :],
+                        out=out[c * P : (c + 1) * P, lo * GW : (hi + 1) * GW],
+                        in_=o[:, c, : (hi - lo + 1) * GW],
                     )
 
-        stage_x(0)
-        stage_x(1)
-        stage_a(0)
-        stage_b(0)
-        stage_a(1)
-        for i in range(NG):
-            if i + 2 < NG:
-                stage_x(i + 2)
+        def ok(g):
+            return 0 <= g < NG
+
+        for i in range(-2, NG + 1):
+            if ok(i + 3):
+                stage_x(i + 3)
+            if ok(i + 2):
                 stage_a(i + 2)
-            if i + 1 < NG:
+            if ok(i + 1):
                 stage_b(i + 1)
-            stage_w(i)
-            stage_q(i)
-            stage_mm(i)
-            if i >= 1:
+            if ok(i + 2) and on_scalar(i + 2):
+                stage_wr(i + 2)
+            if ok(i + 1) and not on_scalar(i + 1):
+                stage_wr(i + 1)
+            if ok(i + 1):
+                stage_wq(i + 1)
+            if ok(i):
+                stage_q(i)
+                stage_mm(i)
+            if ok(i - 1):
                 stage_o(i - 1)
-        stage_o(NG - 1)
+            if i >= 1 and i % 2 == 1 and (i + 7) // 2 < NCH:
+                load_w((i + 7) // 2)

@@ -25,6 +25,9 @@ GW = GF * E
 S_EVERY = 4
 STORES = [4, 4, 4, 4, 4, 4, 4, 2, 1, 1]
 NB2 = 4
+GCOLS = GF * B
+SC = 832
+BIG = 3.4e38
 
 
 def tile_densefeaturenumericembedding_kernel(tc, x, w1, b1, w2, b2, out):
@@ -35,6 +38,7 @@ def tile_densefeaturenumericembedding_kernel(tc, x, w1, b1, w2, b2, out):
         wg_pool = ctx.enter_context(tc.tile_pool(name="wg", bufs=4))
         wq_pool = ctx.enter_context(tc.tile_pool(name="wq", bufs=3))
         h_pool = ctx.enter_context(tc.tile_pool(name="h", bufs=3))
+        g_pool = ctx.enter_context(tc.tile_pool(name="g", bufs=4))
         o_pool = ctx.enter_context(tc.tile_pool(name="o", bufs=2))
         ps_x = ctx.enter_context(tc.psum_pool(name="psx", bufs=2))
         ps_o = ctx.enter_context(tc.psum_pool(name="pso", bufs=6))
@@ -125,14 +129,24 @@ def tile_densefeaturenumericembedding_kernel(tc, x, w1, b1, w2, b2, out):
                     )
             at[g] = a
 
-        def stage_b(g):
-            gr = h_pool.tile([P, GF * B, PACK], BF16, name="gr", align_bytes=64)
-            nc.scalar.activation(
-                out=gr[:].rearrange("p (c i) t -> p c t i", i=4),
-                in_=at[g][:].rearrange("p t f b -> p t (f b)").rearrange("p t (c i) -> p c t i", i=4),
-                func=ACT.Relu,
+        def stage_bg(g):
+            gr = g_pool.tile([P, GCOLS, PACK], BF16, name="gr", align_bytes=64)
+            nc.gpsimd.tensor_scalar(
+                out=gr[:, SC:, :],
+                in0=at[g][:].rearrange("p t f b -> p t (f b)")[:, :, SC:].rearrange("p t c -> p c t"),
+                scalar1=BIG,
+                scalar2=0.0,
+                op0=ALU.min,
+                op1=ALU.max,
             )
             gt[g] = gr
+
+        def stage_b(g):
+            nc.scalar.activation(
+                out=gt[g][:, :SC, :].rearrange("p (c i) t -> p c t i", i=4),
+                in_=at[g][:].rearrange("p t f b -> p t (f b)")[:, :, :SC].rearrange("p t (c i) -> p c t i", i=4),
+                func=ACT.Relu,
+            )
 
         def stage_q(g):
             hc = h_pool.tile([P, GF * B], U32, name="hc", align_bytes=64)
@@ -232,6 +246,9 @@ def tile_densefeaturenumericembedding_kernel(tc, x, w1, b1, w2, b2, out):
                 stage_x(i + 3)
             if ok(i + 2):
                 stage_a(i + 2)
+                stage_bg(i + 2)
+            if ok(i - 1):
+                stage_o(i - 1)
             if ok(i + 1):
                 stage_b(i + 1)
             if ok(i + 2) and on_scalar(i + 2):
@@ -243,7 +260,5 @@ def tile_densefeaturenumericembedding_kernel(tc, x, w1, b1, w2, b2, out):
             if ok(i):
                 stage_q(i)
                 stage_mm(i)
-            if ok(i - 1):
-                stage_o(i - 1)
             if i >= 1 and i % 2 == 1 and (i + 7) // 2 < NCH:
                 load_w((i + 7) // 2)

@@ -79,25 +79,28 @@ def tile_densefeaturenumericembedding_kernel(tc, x, w1, b1, w2, b2, out):
         load_b2(2)
         load_b2(3)
 
-        ident_bf = const.tile([P, P], BF16)
-        make_identity(nc, ident_bf[:])
         ident_f = const.tile([P, P], F32)
         make_identity(nc, ident_f[:])
 
         xb, at, gt, hq, wgt, wq, ops, ot = {}, {}, {}, {}, {}, {}, {}, {}
 
+        x_words = x_sb[:].bitcast(F32)
+
         def stage_x(g):
-            ps = ps_x.tile([P, GF, B], BF16, name="xps")
-            for fi in range(GF):
-                f = g * GF + fi
+            ps = ps_x.tile([P, GF // 2, B], F32, name="xps")
+            for q in range(GF // 2):
+                w = g * (GF // 2) + q
                 for c in range(NBC):
                     nc.tensor.transpose(
-                        ps[:, fi, c * P : (c + 1) * P],
-                        x_sb[:, c, f : f + 1].to_broadcast([P, P]),
-                        ident_bf[:],
+                        ps[:, q, c * P : (c + 1) * P],
+                        x_words[:, c, w : w + 1].to_broadcast([P, P]),
+                        ident_f[:],
                     )
             t = h_pool.tile([P, GF, B], BF16, name="xb")
-            nc.scalar.copy(out=t[:], in_=ps[:])
+            nc.scalar.copy(
+                out=t[:].rearrange("p (q e) b -> p q e b", e=2),
+                in_=ps[:].bitcast(BF16).rearrange("p q (b e) -> p q e b", e=2),
+            )
             xb[g] = t
 
         stage_x(0)

@@ -79,31 +79,36 @@ def tile_densefeaturenumericembedding_kernel(tc, x, w1, b1, w2, b2, out):
         load_b2(2)
         load_b2(3)
 
+        ident_bf = const.tile([P, P], BF16)
+        make_identity(nc, ident_bf[:])
         ident_f = const.tile([P, P], F32)
         make_identity(nc, ident_f[:])
 
         xb, at, gt, hq, wgt, wq, ops, ot = {}, {}, {}, {}, {}, {}, {}, {}
 
-        x_words = x_sb[:].bitcast(F32)
+        xr = {}
+
+        def stage_xr(g):
+            r = h_pool.tile([P, NBC, GF, P], BF16, name="xrep")
+            nc.vector.tensor_copy(
+                out=r[:],
+                in_=x_sb[:, :, g * GF : (g + 1) * GF].unsqueeze(3).to_broadcast([P, NBC, GF, P]),
+            )
+            xr[g] = r
 
         def stage_x(g):
-            ps = ps_x.tile([P, GF // 2, B], F32, name="xps")
-            for q in range(GF // 2):
-                w = g * (GF // 2) + q
+            ps = ps_x.tile([P, GF, B], BF16, name="xps")
+            for fi in range(GF):
                 for c in range(NBC):
-                    nc.tensor.transpose(
-                        ps[:, q, c * P : (c + 1) * P],
-                        x_words[:, c, w : w + 1].to_broadcast([P, P]),
-                        ident_f[:],
-                    )
+                    nc.tensor.transpose(ps[:, fi, c * P : (c + 1) * P], xr[g][:, c, fi, :], ident_bf[:])
             t = h_pool.tile([P, GF, B], BF16, name="xb")
-            nc.scalar.copy(
-                out=t[:].rearrange("p (q e) b -> p q e b", e=2),
-                in_=ps[:].bitcast(BF16).rearrange("p q (b e) -> p q e b", e=2),
-            )
+            nc.scalar.copy(out=t[:], in_=ps[:])
             xb[g] = t
 
+        stage_xr(0)
         stage_x(0)
+        stage_xr(1)
+        stage_xr(2)
 
         scal = []
         for src in (w1_sb, b1_sb):
@@ -245,6 +250,8 @@ def tile_densefeaturenumericembedding_kernel(tc, x, w1, b1, w2, b2, out):
             return 0 <= g < NG
 
         for i in range(-2, NG + 1):
+            if ok(i + 5) and i + 5 >= 3:
+                stage_xr(i + 5)
             if ok(i + 3):
                 stage_x(i + 3)
             if ok(i + 2):

@@ -22,7 +22,10 @@ NG = F // GF
 WF = 8
 NCH = F // WF
 GW = GF * E
-S_EVERY = 4
+V_EVERY = 4
+XF = 16
+XG = XF // GF
+NXC = F // XF
 STORES = [4, 4, 4, 4, 4, 4, 4, 2, 1, 1]
 NB2 = 4
 GCOLS = GF * B
@@ -38,6 +41,7 @@ def tile_densefeaturenumericembedding_kernel(tc, x, w1, b1, w2, b2, out):
         wg_pool = ctx.enter_context(tc.tile_pool(name="wg", bufs=4))
         wq_pool = ctx.enter_context(tc.tile_pool(name="wq", bufs=3))
         h_pool = ctx.enter_context(tc.tile_pool(name="h", bufs=3))
+        x_pool = ctx.enter_context(tc.tile_pool(name="xc", bufs=3))
         g_pool = ctx.enter_context(tc.tile_pool(name="g", bufs=4))
         o_pool = ctx.enter_context(tc.tile_pool(name="o", bufs=2))
         ps_x = ctx.enter_context(tc.psum_pool(name="psx", bufs=2))
@@ -72,12 +76,6 @@ def tile_densefeaturenumericembedding_kernel(tc, x, w1, b1, w2, b2, out):
         nc.sync.dma_start(out=b1_sb[:], in_=b1)
         load_w(0)
         load_w(1)
-        load_b2(0)
-        load_w(2)
-        load_b2(1)
-        load_w(3)
-        load_b2(2)
-        load_b2(3)
 
         ident_bf = const.tile([P, P], BF16)
         make_identity(nc, ident_bf[:])
@@ -86,29 +84,46 @@ def tile_densefeaturenumericembedding_kernel(tc, x, w1, b1, w2, b2, out):
 
         xb, at, gt, hq, wgt, wq, ops, ot = {}, {}, {}, {}, {}, {}, {}, {}
 
-        xr = {}
+        xt_ps = ps_x.tile([P, B], BF16, name="xps")
+        for c in range(NBC):
+            nc.tensor.transpose(xt_ps[:, c * P : (c + 1) * P], x_sb[:, c, :], ident_bf[:])
+        xt_sb = const.tile([P, B], BF16)
+        nc.scalar.copy(out=xt_sb[:], in_=xt_ps[:])
+        park = out[B - 1, :]
+        nc.sync.dma_start(out=park.rearrange("(f w) -> f w", w=B // 2), in_=xt_sb[:].bitcast(F32))
+        xc = {}
 
-        def stage_xr(g):
-            r = h_pool.tile([P, NBC, GF, P], BF16, name="xrep")
-            nc.vector.tensor_copy(
-                out=r[:],
-                in_=x_sb[:, :, g * GF : (g + 1) * GF].unsqueeze(3).to_broadcast([P, NBC, GF, P]),
+        def load_x(j):
+            t = x_pool.tile([P, XF, B], BF16, name="xc")
+            n = XF * B // 2
+            nc.sync.dma_start(
+                out=t[:].rearrange("p f b -> p (f b)").bitcast(F32),
+                in_=park[j * n : (j + 1) * n].partition_broadcast(P),
             )
-            xr[g] = r
+            xc[j] = t
+
+        load_x(1)
+        load_b2(0)
+        load_w(2)
+        load_w(3)
+        load_x(2)
+        load_b2(1)
 
         def stage_x(g):
             ps = ps_x.tile([P, GF, B], BF16, name="xps")
             for fi in range(GF):
+                f = g * GF + fi
                 for c in range(NBC):
-                    nc.tensor.transpose(ps[:, fi, c * P : (c + 1) * P], xr[g][:, c, fi, :], ident_bf[:])
+                    nc.tensor.transpose(
+                        ps[:, fi, c * P : (c + 1) * P],
+                        x_sb[:, c, f : f + 1].to_broadcast([P, P]),
+                        ident_bf[:],
+                    )
             t = h_pool.tile([P, GF, B], BF16, name="xb")
             nc.scalar.copy(out=t[:], in_=ps[:])
             xb[g] = t
 
-        stage_xr(0)
         stage_x(0)
-        stage_xr(1)
-        stage_xr(2)
 
         scal = []
         for src in (w1_sb, b1_sb):
@@ -129,7 +144,7 @@ def tile_densefeaturenumericembedding_kernel(tc, x, w1, b1, w2, b2, out):
                     f = g * GF + fi
                     nc.vector.tensor_scalar(
                         out=a[:, t, fi, :],
-                        in0=xb[g][:, fi, :],
+                        in0=(xb[g][:, fi, :] if g < XG else xc[g // XG][:, (g % XG) * GF + fi, :]),
                         scalar1=w1T[:, t, f : f + 1],
                         scalar2=b1T[:, t, f : f + 1],
                         op0=ALU.mult,
@@ -167,7 +182,7 @@ def tile_densefeaturenumericembedding_kernel(tc, x, w1, b1, w2, b2, out):
             hq[g] = (hc, hs)
 
         def on_scalar(g):
-            return g % S_EVERY == 0
+            return g % V_EVERY != V_EVERY - 1
 
         def stage_wr(g):
             ch, off = divmod(g * GF, WF)
@@ -250,9 +265,7 @@ def tile_densefeaturenumericembedding_kernel(tc, x, w1, b1, w2, b2, out):
             return 0 <= g < NG
 
         for i in range(-2, NG + 1):
-            if ok(i + 5) and i + 5 >= 3:
-                stage_xr(i + 5)
-            if ok(i + 3):
+            if 0 <= i + 3 < XG:
                 stage_x(i + 3)
             if ok(i + 2):
                 stage_a(i + 2)
@@ -272,3 +285,7 @@ def tile_densefeaturenumericembedding_kernel(tc, x, w1, b1, w2, b2, out):
                 stage_mm(i)
             if i >= 1 and i % 2 == 1 and (i + 7) // 2 < NCH:
                 load_w((i + 7) // 2)
+            if i >= 2 and i % XG == 2 and (i + 10) // XG < NXC:
+                load_x((i + 10) // XG)
+            if i in (4, 12):
+                load_b2(i // 8 + 2)

@@ -22,7 +22,7 @@ NG = F // GF
 WF = 8
 NCH = F // WF
 GW = GF * E
-V_EVERY = 4
+V_OF_8 = (2, 5, 7)
 XF = 16
 XG = XF // GF
 NXC = F // XF
@@ -165,6 +165,13 @@ def tile_densefeaturenumericembedding_kernel(tc, x, w1, b1, w2, b2, out):
             gt[g] = gr
 
         def stage_b(g):
+            if g == NG - 1:
+                nc.vector.tensor_scalar_max(
+                    out=gt[g][:, :SC, :].rearrange("p (c i) t -> p c t i", i=4),
+                    in0=at[g][:].rearrange("p t f b -> p t (f b)")[:, :, :SC].rearrange("p t (c i) -> p c t i", i=4),
+                    scalar1=0.0,
+                )
+                return
             nc.scalar.activation(
                 out=gt[g][:, :SC, :].rearrange("p (c i) t -> p c t i", i=4),
                 in_=at[g][:].rearrange("p t f b -> p t (f b)")[:, :, :SC].rearrange("p t (c i) -> p c t i", i=4),
@@ -182,7 +189,7 @@ def tile_densefeaturenumericembedding_kernel(tc, x, w1, b1, w2, b2, out):
             hq[g] = (hc, hs)
 
         def on_scalar(g):
-            return g % V_EVERY != V_EVERY - 1
+            return g % 8 not in V_OF_8
 
         def stage_wr(g):
             ch, off = divmod(g * GF, WF)
@@ -270,8 +277,6 @@ def tile_densefeaturenumericembedding_kernel(tc, x, w1, b1, w2, b2, out):
             if ok(i + 2):
                 stage_a(i + 2)
                 stage_bg(i + 2)
-            if ok(i - 1):
-                stage_o(i - 1)
             if ok(i + 1):
                 stage_b(i + 1)
             if ok(i + 2) and on_scalar(i + 2):
@@ -280,6 +285,8 @@ def tile_densefeaturenumericembedding_kernel(tc, x, w1, b1, w2, b2, out):
                 stage_wr(i + 1)
             if ok(i + 1):
                 stage_wq(i + 1)
+            if ok(i - 1):
+                stage_o(i - 1)
             if ok(i):
                 stage_q(i)
                 stage_mm(i)

@@ -41,6 +41,7 @@ def tile_densefeaturenumericembedding_kernel(tc, x, w1, b1, w2, b2, out):
         wg_pool = ctx.enter_context(tc.tile_pool(name="wg", bufs=4))
         wq_pool = ctx.enter_context(tc.tile_pool(name="wq", bufs=3))
         h_pool = ctx.enter_context(tc.tile_pool(name="h", bufs=3))
+        xh_pool = ctx.enter_context(tc.tile_pool(name="xh", bufs=2))
         x_pool = ctx.enter_context(tc.tile_pool(name="xc", bufs=3))
         g_pool = ctx.enter_context(tc.tile_pool(name="g", bufs=4))
         o_pool = ctx.enter_context(tc.tile_pool(name="o", bufs=2))
@@ -109,33 +110,42 @@ def tile_densefeaturenumericembedding_kernel(tc, x, w1, b1, w2, b2, out):
         load_x(2)
         load_b2(1)
 
+        xr = {}
+
+        def stage_xr(g):
+            r = xh_pool.tile([P, NBC, GF, P], BF16, name="xrep")
+            nc.vector.tensor_copy(
+                out=r[:],
+                in_=x_sb[:, :, g * GF : (g + 1) * GF].unsqueeze(3).to_broadcast([P, NBC, GF, P]),
+            )
+            xr[g] = r
+
         def stage_x(g):
             ps = ps_x.tile([P, GF, B], BF16, name="xps")
             for fi in range(GF):
-                f = g * GF + fi
                 for c in range(NBC):
-                    nc.tensor.transpose(
-                        ps[:, fi, c * P : (c + 1) * P],
-                        x_sb[:, c, f : f + 1].to_broadcast([P, P]),
-                        ident_bf[:],
-                    )
-            t = h_pool.tile([P, GF, B], BF16, name="xb")
+                    nc.tensor.transpose(ps[:, fi, c * P : (c + 1) * P], xr[g][:, c, fi, :], ident_bf[:])
+            t = xh_pool.tile([P, GF, B], BF16, name="xb")
             nc.scalar.copy(out=t[:], in_=ps[:])
             xb[g] = t
 
+        stage_xr(0)
+        w1r = const.tile([P, PACK, P], F32)
+        nc.vector.tensor_copy(out=w1r[:], in_=w1_sb[:].rearrange("f (p t) -> f t p", t=PACK))
+        b1r = const.tile([P, PACK, P], F32)
+        nc.scalar.copy(out=b1r[:], in_=b1_sb[:].rearrange("f (p t) -> f t p", t=PACK))
         stage_x(0)
-
-        scal = []
-        for src in (w1_sb, b1_sb):
-            r = const.tile([P, PACK, P], F32, name="wr32", tag="wr32_%d" % len(scal))
-            nc.vector.tensor_copy(out=r[:], in_=src[:].rearrange("f (p t) -> f t p", t=PACK))
-            ps = ps_o.tile([P, PACK, P], F32, name="po", tag="po")
-            for t in range(PACK):
-                nc.tensor.transpose(ps[:, t, :], r[:, t, :], ident_f[:])
-            s = const.tile([P, PACK, F], F32, name="scalT", tag="scalT_%d" % len(scal))
-            nc.vector.tensor_copy(out=s[:], in_=ps[:])
-            scal.append(s)
-        w1T, b1T = scal
+        stage_xr(1)
+        w1ps = ps_o.tile([P, PACK, P], F32, name="po", tag="po")
+        for t in range(PACK):
+            nc.tensor.transpose(w1ps[:, t, :], w1r[:, t, :], ident_f[:])
+        b1ps = ps_o.tile([P, PACK, P], F32, name="po", tag="po")
+        for t in range(PACK):
+            nc.tensor.transpose(b1ps[:, t, :], b1r[:, t, :], ident_f[:])
+        w1T = const.tile([P, PACK, F], F32)
+        nc.vector.tensor_copy(out=w1T[:], in_=w1ps[:])
+        b1T = const.tile([P, PACK, F], F32)
+        nc.scalar.copy(out=b1T[:], in_=b1ps[:])
 
         def stage_a(g):
             a = h_pool.tile([P, PACK, GF, B], BF16, name="a")
@@ -272,6 +282,8 @@ def tile_densefeaturenumericembedding_kernel(tc, x, w1, b1, w2, b2, out):
             return 0 <= g < NG
 
         for i in range(-2, NG + 1):
+            if 2 <= i + 4 < XG:
+                stage_xr(i + 4)
             if 0 <= i + 3 < XG:
                 stage_x(i + 3)
             if ok(i + 2):

@@ -22,7 +22,7 @@ NG = F // GF
 WF = 8
 NCH = F // WF
 GW = GF * E
-V_OF_8 = (2, 5, 7)
+V_OF_8 = (1, 3, 5, 7)
 XF = 16
 XG = XF // GF
 NXC = F // XF

@@ -289,6 +289,8 @@ def tile_densefeaturenumericembedding_kernel(tc, x, w1, b1, w2, b2, out):
             if ok(i + 2):
                 stage_a(i + 2)
                 stage_bg(i + 2)
+            if ok(i - 1):
+                stage_o(i - 1)
             if ok(i + 1):
                 stage_b(i + 1)
             if ok(i + 2) and on_scalar(i + 2):
@@ -297,8 +299,6 @@ def tile_densefeaturenumericembedding_kernel(tc, x, w1, b1, w2, b2, out):
                 stage_wr(i + 1)
             if ok(i + 1):
                 stage_wq(i + 1)
-            if ok(i - 1):
-                stage_o(i - 1)
             if ok(i):
                 stage_q(i)
                 stage_mm(i)

@@ -297,11 +297,11 @@ def tile_densefeaturenumericembedding_kernel(tc, x, w1, b1, w2, b2, out):
                 stage_wr(i + 2)
             if ok(i + 1) and not on_scalar(i + 1):
                 stage_wr(i + 1)
-            if ok(i + 1):
-                stage_wq(i + 1)
             if ok(i):
                 stage_q(i)
                 stage_mm(i)
+            if ok(i + 1):
+                stage_wq(i + 1)
             if i >= 1 and i % 2 == 1 and (i + 7) // 2 < NCH:
                 load_w((i + 7) // 2)
             if i >= 2 and i % XG == 2 and (i + 10) // XG < NXC:

@@ -29,7 +29,7 @@ NXC = F // XF
 STORES = [4, 4, 4, 4, 4, 4, 4, 2, 1, 1]
 NB2 = 4
 GCOLS = GF * B
-SC = 832
+SC = 864
 BIG = 3.4e38
 
 

@@ -29,7 +29,7 @@ NXC = F // XF
 STORES = [4, 4, 4, 4, 4, 4, 4, 2, 1, 1]
 NB2 = 4
 GCOLS = GF * B
-SC = 864
+SC = 832
 BIG = 3.4e38
 
 
@@ -289,19 +289,16 @@ def tile_densefeaturenumericembedding_kernel(tc, x, w1, b1, w2, b2, out):
             if ok(i + 2):
                 stage_a(i + 2)
                 stage_bg(i + 2)
+            if ok(i):
+                stage_q(i)
+                stage_mm(i)
             if ok(i - 1):
                 stage_o(i - 1)
             if ok(i + 1):
                 stage_b(i + 1)
-            if ok(i + 2) and on_scalar(i + 2):
-                stage_wr(i + 2)
-            if ok(i + 1) and not on_scalar(i + 1):
-                stage_wr(i + 1)
-            if ok(i):
-                stage_q(i)
-                stage_mm(i)
-            if ok(i + 1):
                 stage_wq(i + 1)
+            if ok(i + 2):
+                stage_wr(i + 2)
             if i >= 1 and i % 2 == 1 and (i + 7) // 2 < NCH:
                 load_w((i + 7) // 2)
             if i >= 2 and i % XG == 2 and (i + 10) // XG < NXC:

@@ -26,6 +26,7 @@ V_OF_8 = (1, 3, 5, 7)
 XF = 16
 XG = XF // GF
 NXC = F // XF
+XPE = 2
 STORES = [4, 4, 4, 4, 4, 4, 4, 2, 1, 1]
 NB2 = 4
 GCOLS = GF * B
@@ -94,15 +95,16 @@ def tile_densefeaturenumericembedding_kernel(tc, x, w1, b1, w2, b2, out):
         nc.sync.dma_start(out=park.rearrange("(f w) -> f w", w=B // 2), in_=xt_sb[:].bitcast(F32))
         xc = {}
 
-        def load_x(j):
+        def load_x(j, first=0):
             t = x_pool.tile([P, XF, B], BF16, name="xc")
-            n = XF * B // 2
+            n = B // 2
             nc.sync.dma_start(
-                out=t[:].rearrange("p f b -> p (f b)").bitcast(F32),
-                in_=park[j * n : (j + 1) * n].partition_broadcast(P),
+                out=t[:, first:, :].rearrange("p f b -> p (f b)").bitcast(F32),
+                in_=park[(j * XF + first) * n : (j + 1) * XF * n].partition_broadcast(P),
             )
             xc[j] = t
 
+        load_x(0, first=XPE * GF)
         load_x(1)
         load_b2(0)
         load_w(2)
@@ -154,7 +156,7 @@ def tile_densefeaturenumericembedding_kernel(tc, x, w1, b1, w2, b2, out):
                     f = g * GF + fi
                     nc.vector.tensor_scalar(
                         out=a[:, t, fi, :],
-                        in0=(xb[g][:, fi, :] if g < XG else xc[g // XG][:, (g % XG) * GF + fi, :]),
+                        in0=(xb[g][:, fi, :] if g < XPE else xc[g // XG][:, (g % XG) * GF + fi, :]),
                         scalar1=w1T[:, t, f : f + 1],
                         scalar2=b1T[:, t, f : f + 1],
                         op0=ALU.mult,
@@ -282,9 +284,9 @@ def tile_densefeaturenumericembedding_kernel(tc, x, w1, b1, w2, b2, out):
             return 0 <= g < NG
 
         for i in range(-2, NG + 1):
-            if 2 <= i + 4 < XG:
+            if 2 <= i + 4 < XPE:
                 stage_xr(i + 4)
-            if 0 <= i + 3 < XG:
+            if 0 <= i + 3 < XPE:
                 stage_x(i + 3)
             if ok(i + 2):
                 stage_a(i + 2)

@@ -177,13 +177,6 @@ def tile_densefeaturenumericembedding_kernel(tc, x, w1, b1, w2, b2, out):
             gt[g] = gr
 
         def stage_b(g):
-            if g == NG - 1:
-                nc.vector.tensor_scalar_max(
-                    out=gt[g][:, :SC, :].rearrange("p (c i) t -> p c t i", i=4),
-                    in0=at[g][:].rearrange("p t f b -> p t (f b)")[:, :, :SC].rearrange("p t (c i) -> p c t i", i=4),
-                    scalar1=0.0,
-                )
-                return
             nc.scalar.activation(
                 out=gt[g][:, :SC, :].rearrange("p (c i) t -> p c t i", i=4),
                 in_=at[g][:].rearrange("p t f b -> p t (f b)")[:, :, :SC].rearrange("p t (c i) -> p c t i", i=4),

@@ -167,8 +167,8 @@ def tile_densefeaturenumericembedding_kernel(tc, x, w1, b1, w2, b2, out):
         def stage_bg(g):
             gr = g_pool.tile([P, GCOLS, PACK], BF16, name="gr", align_bytes=64)
             nc.gpsimd.tensor_scalar(
-                out=gr[:, SC:, :],
-                in0=at[g][:].rearrange("p t f b -> p t (f b)")[:, :, SC:].rearrange("p t c -> p c t"),
+                out=gr[:, SC:, :].rearrange("p (c i) t -> p c t i", i=4),
+                in0=at[g][:].rearrange("p t f b -> p t (f b)")[:, :, SC:].rearrange("p t (c i) -> p c t i", i=4),
                 scalar1=BIG,
                 scalar2=0.0,
                 op0=ALU.min,

@@ -22,7 +22,7 @@ NG = F // GF
 WF = 8
 NCH = F // WF
 GW = GF * E
-V_OF_8 = (1, 3, 5, 7)
+WS = 2
 XF = 16
 XG = XF // GF
 NXC = F // XF
@@ -193,23 +193,17 @@ def tile_densefeaturenumericembedding_kernel(tc, x, w1, b1, w2, b2, out):
             )
             hq[g] = (hc, hs)
 
-        def on_scalar(g):
-            return g % 8 not in V_OF_8
-
         def stage_wr(g):
             ch, off = divmod(g * GF, WF)
             wg = wg_pool.tile([P, GF, E, PACK], BF16, name="wg", align_bytes=64)
-            if on_scalar(g):
-                for fi in range(GF):
-                    nc.scalar.copy(
-                        out=wg[:, fi].rearrange("p (c i) t -> p c t i", i=4),
-                        in_=wraw[ch][:, off + fi, :].rearrange("p (t c i) -> p c t i", t=PACK, i=4),
-                    )
-            else:
-                nc.vector.tensor_copy(
-                    out=wg[:].rearrange("p f (c i) t -> p f c t i", i=4),
-                    in_=wraw[ch][:, off : off + GF, :].rearrange("p f (t c i) -> p f c t i", t=PACK, i=4),
-                )
+            nc.scalar.copy(
+                out=wg[:, :WS].rearrange("p f (c i) t -> p f c t i", i=4),
+                in_=wraw[ch][:, off : off + WS, :].rearrange("p f (t c i) -> p f c t i", t=PACK, i=4),
+            )
+            nc.vector.tensor_copy(
+                out=wg[:, WS:].rearrange("p f (c i) t -> p f c t i", i=4),
+                in_=wraw[ch][:, off + WS : off + GF, :].rearrange("p f (t c i) -> p f c t i", t=PACK, i=4),
+            )
             wgt[g] = wg
 
         def stage_wq(g):

@@ -22,11 +22,13 @@ NG = F // GF
 WF = 8
 NCH = F // WF
 GW = GF * E
-WS = 2
+ES = 60
 XF = 16
 XG = XF // GF
 NXC = F // XF
-XPE = 2
+NPE = 3
+PF = NPE * GF
+HALF = P // 2
 STORES = [4, 4, 4, 4, 4, 4, 4, 2, 1, 1]
 NB2 = 4
 GCOLS = GF * B
@@ -42,12 +44,11 @@ def tile_densefeaturenumericembedding_kernel(tc, x, w1, b1, w2, b2, out):
         wg_pool = ctx.enter_context(tc.tile_pool(name="wg", bufs=4))
         wq_pool = ctx.enter_context(tc.tile_pool(name="wq", bufs=3))
         h_pool = ctx.enter_context(tc.tile_pool(name="h", bufs=3))
-        xh_pool = ctx.enter_context(tc.tile_pool(name="xh", bufs=2))
         x_pool = ctx.enter_context(tc.tile_pool(name="xc", bufs=3))
         g_pool = ctx.enter_context(tc.tile_pool(name="g", bufs=4))
         o_pool = ctx.enter_context(tc.tile_pool(name="o", bufs=2))
-        ps_x = ctx.enter_context(tc.psum_pool(name="psx", bufs=2))
-        ps_o = ctx.enter_context(tc.psum_pool(name="pso", bufs=6))
+        ps_a = ctx.enter_context(tc.psum_pool(name="psa", bufs=4))
+        ps_o = ctx.enter_context(tc.psum_pool(name="pso", bufs=4))
         ctx.enter_context(tc.manual_schedule())
 
         wraw = {}
@@ -72,21 +73,22 @@ def tile_densefeaturenumericembedding_kernel(tc, x, w1, b1, w2, b2, out):
 
         x_sb = const.tile([P, NBC, F], BF16)
         nc.sync.dma_start(out=x_sb[:], in_=x.rearrange("(c p) f -> p c f", p=P))
+        wb = const.tile([P, H], BF16)
+        nc.sync.dma_start(out=wb[:HALF, :], in_=w1[:HALF, :])
+        nc.sync.dma_start(out=wb[HALF:, :], in_=b1[:HALF, :])
+        load_w(0)
         w1_sb = const.tile([P, H], BF16)
         nc.sync.dma_start(out=w1_sb[:], in_=w1)
         b1_sb = const.tile([P, H], BF16)
         nc.sync.dma_start(out=b1_sb[:], in_=b1)
-        load_w(0)
         load_w(1)
 
         ident_bf = const.tile([P, P], BF16)
         make_identity(nc, ident_bf[:])
-        ident_f = const.tile([P, P], F32)
-        make_identity(nc, ident_f[:])
 
-        xb, at, gt, hq, wgt, wq, ops, ot = {}, {}, {}, {}, {}, {}, {}, {}
+        at, gt, hq, wgt, wq, ops, ot = {}, {}, {}, {}, {}, {}, {}
 
-        xt_ps = ps_x.tile([P, B], BF16, name="xps")
+        xt_ps = ps_a.tile([P, B], BF16, name="pa")
         for c in range(NBC):
             nc.tensor.transpose(xt_ps[:, c * P : (c + 1) * P], x_sb[:, c, :], ident_bf[:])
         xt_sb = const.tile([P, B], BF16)
@@ -104,7 +106,7 @@ def tile_densefeaturenumericembedding_kernel(tc, x, w1, b1, w2, b2, out):
             )
             xc[j] = t
 
-        load_x(0, first=XPE * GF)
+        load_x(0, first=PF)
         load_x(1)
         load_b2(0)
         load_w(2)
@@ -112,42 +114,55 @@ def tile_densefeaturenumericembedding_kernel(tc, x, w1, b1, w2, b2, out):
         load_x(2)
         load_b2(1)
 
-        xr = {}
-
-        def stage_xr(g):
-            r = xh_pool.tile([P, NBC, GF, P], BF16, name="xrep")
-            nc.vector.tensor_copy(
-                out=r[:],
-                in_=x_sb[:, :, g * GF : (g + 1) * GF].unsqueeze(3).to_broadcast([P, NBC, GF, P]),
+        xs = const.tile([P, PF, B], BF16)
+        for j in range(PF):
+            nc.vector.tensor_scalar(
+                out=xs[:, j, :],
+                in0=xt_sb[:],
+                scalar1=ident_bf[:, j : j + 1],
+                scalar2=ident_bf[:, HALF + j : HALF + j + 1],
+                op0=ALU.mult,
+                op1=ALU.add,
             )
-            xr[g] = r
+        wbv = wb[:].rearrange("r (p t) -> r t p", t=PACK)
 
-        def stage_x(g):
-            ps = ps_x.tile([P, GF, B], BF16, name="xps")
+        def stage_pb(g):
+            gr = g_pool.tile([P, GCOLS, PACK], BF16, name="gr", align_bytes=64)
             for fi in range(GF):
+                banks = []
                 for c in range(NBC):
-                    nc.tensor.transpose(ps[:, fi, c * P : (c + 1) * P], xr[g][:, c, fi, :], ident_bf[:])
-            t = xh_pool.tile([P, GF, B], BF16, name="xb")
-            nc.scalar.copy(out=t[:], in_=ps[:])
-            xb[g] = t
+                    bank = ps_a.tile([P, PACK, P], F32, name="pa")
+                    banks.append(bank)
+                for t in range(PACK):
+                    for c in range(NBC):
+                        nc.tensor.matmul(
+                            out=banks[c][:, t, :],
+                            lhsT=wbv[:, t, :],
+                            rhs=xs[:, g * GF + fi, c * P : (c + 1) * P],
+                            start=True,
+                            stop=True,
+                        )
+                for c in range(NBC):
+                    col = fi * B + c * P
+                    nc.scalar.activation(
+                        out=gr[:, col : col + P, :],
+                        in_=banks[c][:].rearrange("p t b -> p b t"),
+                        func=ACT.Relu,
+                    )
+            gt[g] = gr
 
-        stage_xr(0)
-        w1r = const.tile([P, PACK, P], F32)
-        nc.vector.tensor_copy(out=w1r[:], in_=w1_sb[:].rearrange("f (p t) -> f t p", t=PACK))
-        b1r = const.tile([P, PACK, P], F32)
-        nc.scalar.copy(out=b1r[:], in_=b1_sb[:].rearrange("f (p t) -> f t p", t=PACK))
-        stage_x(0)
-        stage_xr(1)
-        w1ps = ps_o.tile([P, PACK, P], F32, name="po", tag="po")
-        for t in range(PACK):
-            nc.tensor.transpose(w1ps[:, t, :], w1r[:, t, :], ident_f[:])
-        b1ps = ps_o.tile([P, PACK, P], F32, name="po", tag="po")
-        for t in range(PACK):
-            nc.tensor.transpose(b1ps[:, t, :], b1r[:, t, :], ident_f[:])
         w1T = const.tile([P, PACK, F], F32)
-        nc.vector.tensor_copy(out=w1T[:], in_=w1ps[:])
         b1T = const.tile([P, PACK, F], F32)
-        nc.scalar.copy(out=b1T[:], in_=b1ps[:])
+
+        def stage_scalars():
+            w1ps = ps_a.tile([P, PACK, P], BF16, name="pa")
+            for t in range(PACK):
+                nc.tensor.transpose(w1ps[:, t, :], w1_sb[:].rearrange("f (p t) -> f t p", t=PACK)[:, t, :], ident_bf[:])
+            nc.vector.tensor_copy(out=w1T[:], in_=w1ps[:])
+            b1ps = ps_a.tile([P, PACK, P], BF16, name="pa")
+            for t in range(PACK):
+                nc.tensor.transpose(b1ps[:, t, :], b1_sb[:].rearrange("f (p t) -> f t p", t=PACK)[:, t, :], ident_bf[:])
+            nc.scalar.copy(out=b1T[:], in_=b1ps[:])
 
         def stage_a(g):
             a = h_pool.tile([P, PACK, GF, B], BF16, name="a")
@@ -156,7 +171,7 @@ def tile_densefeaturenumericembedding_kernel(tc, x, w1, b1, w2, b2, out):
                     f = g * GF + fi
                     nc.vector.tensor_scalar(
                         out=a[:, t, fi, :],
-                        in0=(xb[g][:, fi, :] if g < XPE else xc[g // XG][:, (g % XG) * GF + fi, :]),
+                        in0=xc[g // XG][:, (g % XG) * GF + fi, :],
                         scalar1=w1T[:, t, f : f + 1],
                         scalar2=b1T[:, t, f : f + 1],
                         op0=ALU.mult,
@@ -196,13 +211,16 @@ def tile_densefeaturenumericembedding_kernel(tc, x, w1, b1, w2, b2, out):
         def stage_wr(g):
             ch, off = divmod(g * GF, WF)
             wg = wg_pool.tile([P, GF, E, PACK], BF16, name="wg", align_bytes=64)
-            nc.scalar.copy(
-                out=wg[:, :WS].rearrange("p f (c i) t -> p f c t i", i=4),
-                in_=wraw[ch][:, off : off + WS, :].rearrange("p f (t c i) -> p f c t i", t=PACK, i=4),
-            )
+            raw = wraw[ch][:, off : off + GF, :].rearrange("p f (t e) -> p f t e", t=PACK)
+            es = ES if g >= NPE else 0
+            if es > 0:
+                nc.scalar.copy(
+                    out=wg[:, :, :es, :].rearrange("p f (c i) t -> p f c t i", i=4),
+                    in_=raw[:, :, :, :es].rearrange("p f t (c i) -> p f c t i", i=4),
+                )
             nc.vector.tensor_copy(
-                out=wg[:, WS:].rearrange("p f (c i) t -> p f c t i", i=4),
-                in_=wraw[ch][:, off + WS : off + GF, :].rearrange("p f (t c i) -> p f c t i", t=PACK, i=4),
+                out=wg[:, :, es:, :].rearrange("p f (c i) t -> p f c t i", i=4),
+                in_=raw[:, :, :, es:].rearrange("p f t (c i) -> p f c t i", i=4),
             )
             wgt[g] = wg
 
@@ -271,20 +289,23 @@ def tile_densefeaturenumericembedding_kernel(tc, x, w1, b1, w2, b2, out):
             return 0 <= g < NG
 
         for i in range(-2, NG + 1):
-            if 2 <= i + 4 < XPE:
-                stage_xr(i + 4)
-            if 0 <= i + 3 < XPE:
-                stage_x(i + 3)
-            if ok(i + 2):
+            if NPE <= i + 2 < NG:
                 stage_a(i + 2)
                 stage_bg(i + 2)
+            if i == -2:
+                stage_pb(0)
+            if i == -1:
+                stage_scalars()
+            if 1 <= i + 1 < NPE:
+                stage_pb(i + 1)
             if ok(i):
                 stage_q(i)
                 stage_mm(i)
             if ok(i - 1):
                 stage_o(i - 1)
             if ok(i + 1):
-                stage_b(i + 1)
+                if i + 1 >= NPE:
+                    stage_b(i + 1)
                 stage_wq(i + 1)
             if ok(i + 2):
                 stage_wr(i + 2)

@@ -22,7 +22,7 @@ NG = F // GF
 WF = 8
 NCH = F // WF
 GW = GF * E
-ES = 60
+ES = 72
 XF = 16
 XG = XF // GF
 NXC = F // XF

@@ -34,6 +34,7 @@ NB2 = 4
 GCOLS = GF * B
 SC = 832
 BIG = 3.4e38
+RS = 8
 
 
 def tile_densefeaturenumericembedding_kernel(tc, x, w1, b1, w2, b2, out):
@@ -193,8 +194,8 @@ def tile_densefeaturenumericembedding_kernel(tc, x, w1, b1, w2, b2, out):
 
         def stage_b(g):
             nc.scalar.activation(
-                out=gt[g][:, :SC, :].rearrange("p (c i) t -> p c t i", i=4),
-                in_=at[g][:].rearrange("p t f b -> p t (f b)")[:, :, :SC].rearrange("p t (c i) -> p c t i", i=4),
+                out=gt[g][:, :SC, :].rearrange("p (c i) t -> p c t i", i=RS),
+                in_=at[g][:].rearrange("p t f b -> p t (f b)")[:, :, :SC].rearrange("p t (c i) -> p c t i", i=RS),
                 func=ACT.Relu,
             )
 
@@ -215,8 +216,8 @@ def tile_densefeaturenumericembedding_kernel(tc, x, w1, b1, w2, b2, out):
             es = ES if g >= NPE else 0
             if es > 0:
                 nc.scalar.copy(
-                    out=wg[:, :, :es, :].rearrange("p f (c i) t -> p f c t i", i=4),
-                    in_=raw[:, :, :, :es].rearrange("p f t (c i) -> p f c t i", i=4),
+                    out=wg[:, :, :es, :].rearrange("p f (c i) t -> p f c t i", i=RS),
+                    in_=raw[:, :, :, :es].rearrange("p f t (c i) -> p f c t i", i=RS),
                 )
             nc.vector.tensor_copy(
                 out=wg[:, :, es:, :].rearrange("p f (c i) t -> p f c t i", i=4),

@@ -34,6 +34,8 @@ NB2 = 4
 GCOLS = GF * B
 SC = 832
 BIG = 3.4e38
+LAST = NG - 1
+HF = GF // 2
 RS = 8
 
 
@@ -166,13 +168,13 @@ def tile_densefeaturenumericembedding_kernel(tc, x, w1, b1, w2, b2, out):
             nc.scalar.copy(out=b1T[:], in_=b1ps[:])
 
         def stage_a(g):
-            a = h_pool.tile([P, PACK, GF, B], BF16, name="a")
+            a = h_pool.tile([P, GF, B // RS, PACK, RS], BF16, name="a", align_bytes=64)
             for t in range(PACK):
                 for fi in range(GF):
                     f = g * GF + fi
                     nc.vector.tensor_scalar(
-                        out=a[:, t, fi, :],
-                        in0=xc[g // XG][:, (g % XG) * GF + fi, :],
+                        out=a[:, fi, :, t, :],
+                        in0=xc[g // XG][:, (g % XG) * GF + fi, :].rearrange("p (c i) -> p c i", i=RS),
                         scalar1=w1T[:, t, f : f + 1],
                         scalar2=b1T[:, t, f : f + 1],
                         op0=ALU.mult,
@@ -183,8 +185,8 @@ def tile_densefeaturenumericembedding_kernel(tc, x, w1, b1, w2, b2, out):
         def stage_bg(g):
             gr = g_pool.tile([P, GCOLS, PACK], BF16, name="gr", align_bytes=64)
             nc.gpsimd.tensor_scalar(
-                out=gr[:, SC:, :].rearrange("p (c i) t -> p c t i", i=4),
-                in0=at[g][:].rearrange("p t f b -> p t (f b)")[:, :, SC:].rearrange("p t (c i) -> p c t i", i=4),
+                out=gr[:, SC:, :].rearrange("p (c i) t -> p c t i", i=RS),
+                in0=at[g][:].rearrange("p f c t i -> p (f c) t i")[:, SC // RS :, :, :],
                 scalar1=BIG,
                 scalar2=0.0,
                 op0=ALU.min,
@@ -193,11 +195,13 @@ def tile_densefeaturenumericembedding_kernel(tc, x, w1, b1, w2, b2, out):
             gt[g] = gr
 
         def stage_b(g):
-            nc.scalar.activation(
-                out=gt[g][:, :SC, :].rearrange("p (c i) t -> p c t i", i=RS),
-                in_=at[g][:].rearrange("p t f b -> p t (f b)")[:, :, :SC].rearrange("p t (c i) -> p c t i", i=RS),
-                func=ACT.Relu,
-            )
+            cuts = [0, SC] if g < LAST else [0, HF * B, SC]
+            for lo, hi in zip(cuts[:-1], cuts[1:]):
+                nc.scalar.activation(
+                    out=gt[g][:, lo:hi, :].rearrange("p (c i) t -> p c t i", i=RS),
+                    in_=at[g][:].rearrange("p f c t i -> p (f c) t i")[:, lo // RS : hi // RS, :, :],
+                    func=ACT.Relu,
+                )
 
         def stage_q(g):
             hc = h_pool.tile([P, GF * B], U32, name="hc", align_bytes=64)
@@ -286,6 +290,55 @@ def tile_densefeaturenumericembedding_kernel(tc, x, w1, b1, w2, b2, out):
                         in_=o[:, c, : (hi - lo + 1) * GW],
                     )
 
+        tail = {}
+
+        def tail_q(h):
+            if h == 0:
+                tail["hc"] = h_pool.tile([P, GF * B], U32, name="hc", align_bytes=64)
+                tail["hs"] = h_pool.tile([P, GF * B], U8, name="hs", align_bytes=64)
+            cols = slice(h * HF * B, (h + 1) * HF * B)
+            nc.vector.quantize_mx(
+                out=tail["hc"][:, cols].bitcast(FP8X4),
+                scales=tail["hs"][:, cols],
+                in_=gt[LAST][:, cols, :].rearrange("p c t -> p (c t)"),
+            )
+
+        def tail_mm(h):
+            wc, ws = wq[LAST]
+            for c in range(NBC):
+                po = ps_o.tile([P, HF * E], F32, name="po", tag="po")
+                for k in range(HF):
+                    fi = h * HF + k
+                    hcol = slice(fi * B + c * P, fi * B + (c + 1) * P)
+                    wcol = slice(fi * E, (fi + 1) * E)
+                    nc.tensor.matmul_mx(
+                        out=po[:, k * E : (k + 1) * E],
+                        lhsT=tail["hc"][:, hcol].bitcast(FP8X4),
+                        lhsT_scale=tail["hs"][:, hcol],
+                        rhs=wc[:, wcol].bitcast(FP8X4),
+                        rhs_scale=ws[:, wcol],
+                        start=True,
+                        stop=True,
+                    )
+                tail[(h, c)] = po
+
+        def tail_o(h):
+            if h == 0:
+                tail["o"] = o_pool.tile([P, NBC, max(STORES) * GW], F32, name="ot")
+            o = tail["o"]
+            n = HF * E
+            for c in range(NBC):
+                nc.vector.tensor_tensor(
+                    out=o[:, c, h * n : (h + 1) * n],
+                    in0=tail[(h, c)][:],
+                    in1=b2bc[:, LAST * GW + h * n : LAST * GW + (h + 1) * n],
+                    op=ALU.add,
+                )
+                nc.sync.dma_start(
+                    out=out[c * P : (c + 1) * P, LAST * GW + h * n : LAST * GW + (h + 1) * n],
+                    in_=o[:, c, h * n : (h + 1) * n],
+                )
+
         def ok(g):
             return 0 <= g < NG
 
@@ -299,11 +352,20 @@ def tile_densefeaturenumericembedding_kernel(tc, x, w1, b1, w2, b2, out):
                 stage_scalars()
             if 1 <= i + 1 < NPE:
                 stage_pb(i + 1)
-            if ok(i):
+            if 0 <= i < LAST:
                 stage_q(i)
                 stage_mm(i)
-            if ok(i - 1):
+            if i == LAST:
+                tail_q(0)
+                tail_mm(0)
+            if 0 <= i - 1 < LAST:
                 stage_o(i - 1)
+            if i == LAST:
+                tail_q(1)
+                tail_mm(1)
+                tail_o(0)
+            if i - 1 == LAST:
+                tail_o(1)
             if ok(i + 1):
                 if i + 1 >= NPE:
                     stage_b(i + 1)

@@ -324,7 +324,7 @@ def tile_densefeaturenumericembedding_kernel(tc, x, w1, b1, w2, b2, out):
 
         def tail_o(h):
             if h == 0:
-                tail["o"] = o_pool.tile([P, NBC, max(STORES) * GW], F32, name="ot")
+                tail["o"] = const.tile([P, NBC, GW], F32, name="otail")
             o = tail["o"]
             n = HF * E
             for c in range(NBC):

@@ -154,18 +154,17 @@ def tile_densefeaturenumericembedding_kernel(tc, x, w1, b1, w2, b2, out):
                     )
             gt[g] = gr
 
-        w1T = const.tile([P, PACK, F], F32)
-        b1T = const.tile([P, PACK, F], F32)
+        wbT = const.tile([P, PACK, F, 2], F32)
 
         def stage_scalars():
             w1ps = ps_a.tile([P, PACK, P], BF16, name="pa")
             for t in range(PACK):
                 nc.tensor.transpose(w1ps[:, t, :], w1_sb[:].rearrange("f (p t) -> f t p", t=PACK)[:, t, :], ident_bf[:])
-            nc.vector.tensor_copy(out=w1T[:], in_=w1ps[:])
+            nc.vector.tensor_copy(out=wbT[:, :, :, 0], in_=w1ps[:])
             b1ps = ps_a.tile([P, PACK, P], BF16, name="pa")
             for t in range(PACK):
                 nc.tensor.transpose(b1ps[:, t, :], b1_sb[:].rearrange("f (p t) -> f t p", t=PACK)[:, t, :], ident_bf[:])
-            nc.scalar.copy(out=b1T[:], in_=b1ps[:])
+            nc.scalar.copy(out=wbT[:, :, :, 1], in_=b1ps[:])
 
         def stage_a(g):
             a = h_pool.tile([P, GF, B // RS, PACK, RS], BF16, name="a", align_bytes=64)
@@ -175,8 +174,8 @@ def tile_densefeaturenumericembedding_kernel(tc, x, w1, b1, w2, b2, out):
                     nc.vector.tensor_scalar(
                         out=a[:, fi, :, t, :],
                         in0=xc[g // XG][:, (g % XG) * GF + fi, :].rearrange("p (c i) -> p c i", i=RS),
-                        scalar1=w1T[:, t, f : f + 1],
-                        scalar2=b1T[:, t, f : f + 1],
+                        scalar1=wbT[:, t, f, 0:1],
+                        scalar2=wbT[:, t, f, 1:2],
                         op0=ALU.mult,
                         op1=ALU.add,
                     )
@@ -224,8 +223,8 @@ def tile_densefeaturenumericembedding_kernel(tc, x, w1, b1, w2, b2, out):
                     in_=raw[:, :, :, :es].rearrange("p f t (c i) -> p f c t i", i=RS),
                 )
             nc.vector.tensor_copy(
-                out=wg[:, :, es:, :].rearrange("p f (c i) t -> p f c t i", i=4),
-                in_=raw[:, :, :, es:].rearrange("p f t (c i) -> p f c t i", i=4),
+                out=wg[:, :, es:, :].rearrange("p f (c i) t -> p f c t i", i=RS),
+                in_=raw[:, :, :, es:].rearrange("p f t (c i) -> p f c t i", i=RS),
             )
             wgt[g] = wg
 

@@ -157,14 +157,11 @@ def tile_densefeaturenumericembedding_kernel(tc, x, w1, b1, w2, b2, out):
         wbT = const.tile([P, PACK, F, 2], F32)
 
         def stage_scalars():
-            w1ps = ps_a.tile([P, PACK, P], BF16, name="pa")
-            for t in range(PACK):
-                nc.tensor.transpose(w1ps[:, t, :], w1_sb[:].rearrange("f (p t) -> f t p", t=PACK)[:, t, :], ident_bf[:])
-            nc.vector.tensor_copy(out=wbT[:, :, :, 0], in_=w1ps[:])
-            b1ps = ps_a.tile([P, PACK, P], BF16, name="pa")
-            for t in range(PACK):
-                nc.tensor.transpose(b1ps[:, t, :], b1_sb[:].rearrange("f (p t) -> f t p", t=PACK)[:, t, :], ident_bf[:])
-            nc.scalar.copy(out=wbT[:, :, :, 1], in_=b1ps[:])
+            wbps = ps_a.tile([P, 2, PACK, P], BF16, name="pa")
+            for j, rows in enumerate((w1_sb, b1_sb)):
+                for t in range(PACK):
+                    nc.tensor.transpose(wbps[:, j, t, :], rows[:].rearrange("f (p t) -> f t p", t=PACK)[:, t, :], ident_bf[:])
+            nc.vector.tensor_copy(out=wbT[:], in_=wbps[:].rearrange("p j t f -> p t f j"))
 
         def stage_a(g):
             a = h_pool.tile([P, GF, B // RS, PACK, RS], BF16, name="a", align_bytes=64)

from contextlib import ExitStack

import concourse.mybir as mybir
from concourse.masks import make_identity

FLOPS = 2 * 256 * 128 * 512 * 128

BF16 = mybir.dt.bfloat16
F32 = mybir.dt.float32
U32 = mybir.dt.uint32
U8 = mybir.dt.uint8
FP8X4 = mybir.dt.float8_e4m3fn_x4
ALU = mybir.AluOpType
ACT = mybir.ActivationFunctionType

P = 128
PACK = 4
B, F, H, E = 256, 128, 512, 128
NBC = B // P
GF = 4
NG = F // GF
WF = 8
NCH = F // WF
GW = GF * E
ES = 72
XF = 16
XG = XF // GF
NXC = F // XF
NPE = 3
PF = NPE * GF
HALF = P // 2
STORES = [4, 4, 4, 4, 4, 4, 4, 2, 1, 1]
NB2 = 4
GCOLS = GF * B
SC = 832
BIG = 3.4e38
LAST = NG - 1
HF = GF // 2
RS = 8


def tile_densefeaturenumericembedding_kernel(tc, x, w1, b1, w2, b2, out):
    nc = tc.nc
    with ExitStack() as ctx:
        const = ctx.enter_context(tc.tile_pool(name="const", bufs=1))
        wraw_pool = ctx.enter_context(tc.tile_pool(name="wraw", bufs=4))
        wg_pool = ctx.enter_context(tc.tile_pool(name="wg", bufs=4))
        wq_pool = ctx.enter_context(tc.tile_pool(name="wq", bufs=3))
        h_pool = ctx.enter_context(tc.tile_pool(name="h", bufs=3))
        x_pool = ctx.enter_context(tc.tile_pool(name="xc", bufs=3))
        g_pool = ctx.enter_context(tc.tile_pool(name="g", bufs=4))
        o_pool = ctx.enter_context(tc.tile_pool(name="o", bufs=2))
        ps_a = ctx.enter_context(tc.psum_pool(name="psa", bufs=4))
        ps_o = ctx.enter_context(tc.psum_pool(name="pso", bufs=4))
        ctx.enter_context(tc.manual_schedule())

        wraw = {}

        def load_w(ch):
            t = wraw_pool.tile([P, WF, PACK * E], BF16, name="w2raw")
            nc.sync.dma_start(
                out=t[:],
                in_=w2[ch * WF : (ch + 1) * WF].rearrange("f (p j) e -> p f (j e)", j=PACK),
            )
            wraw[ch] = t

        b2bc = const.tile([P, F * E], BF16)
        b2flat = b2.rearrange("f e -> (f e)")

        def load_b2(i):
            n = F * E // NB2
            nc.sync.dma_start(
                out=b2bc[:, i * n : (i + 1) * n],
                in_=b2flat[i * n : (i + 1) * n].partition_broadcast(P),
            )

        x_sb = const.tile([P, NBC, F], BF16)
        nc.sync.dma_start(out=x_sb[:], in_=x.rearrange("(c p) f -> p c f", p=P))
        wb = const.tile([P, H], BF16)
        nc.sync.dma_start(out=wb[:HALF, :], in_=w1[:HALF, :])
        nc.sync.dma_start(out=wb[HALF:, :], in_=b1[:HALF, :])
        load_w(0)
        w1_sb = const.tile([P, H], BF16)
        nc.sync.dma_start(out=w1_sb[:], in_=w1)
        b1_sb = const.tile([P, H], BF16)
        nc.sync.dma_start(out=b1_sb[:], in_=b1)
        load_w(1)

        ident_bf = const.tile([P, P], BF16)
        make_identity(nc, ident_bf[:])

        at, gt, hq, wgt, wq, ops, ot = {}, {}, {}, {}, {}, {}, {}

        xt_ps = ps_a.tile([P, B], BF16, name="pa")
        for c in range(NBC):
            nc.tensor.transpose(xt_ps[:, c * P : (c + 1) * P], x_sb[:, c, :], ident_bf[:])
        xt_sb = const.tile([P, B], BF16)
        nc.scalar.copy(out=xt_sb[:], in_=xt_ps[:])
        park = out[B - 1, :]
        nc.sync.dma_start(out=park.rearrange("(f w) -> f w", w=B // 2), in_=xt_sb[:].bitcast(F32))
        xc = {}

        def load_x(j, first=0):
            t = x_pool.tile([P, XF, B], BF16, name="xc")
            n = B // 2
            nc.sync.dma_start(
                out=t[:, first:, :].rearrange("p f b -> p (f b)").bitcast(F32),
                in_=park[(j * XF + first) * n : (j + 1) * XF * n].partition_broadcast(P),
            )
            xc[j] = t

        load_x(0, first=PF)
        load_x(1)
        load_b2(0)
        load_w(2)
        load_w(3)
        load_x(2)
        load_b2(1)

        xs = const.tile([P, PF, B], BF16)
        for j in range(PF):
            nc.vector.tensor_scalar(
                out=xs[:, j, :],
                in0=xt_sb[:],
                scalar1=ident_bf[:, j : j + 1],
                scalar2=ident_bf[:, HALF + j : HALF + j + 1],
                op0=ALU.mult,
                op1=ALU.add,
            )
        wbv = wb[:].rearrange("r (p t) -> r t p", t=PACK)

        def stage_pb(g):
            gr = g_pool.tile([P, GCOLS, PACK], BF16, name="gr", align_bytes=64)
            for fi in range(GF):
                banks = []
                for c in range(NBC):
                    bank = ps_a.tile([P, PACK, P], F32, name="pa")
                    banks.append(bank)
                for t in range(PACK):
                    for c in range(NBC):
                        nc.tensor.matmul(
                            out=banks[c][:, t, :],
                            lhsT=wbv[:, t, :],
                            rhs=xs[:, g * GF + fi, c * P : (c + 1) * P],
                            start=True,
                            stop=True,
                        )
                for c in range(NBC):
                    col = fi * B + c * P
                    nc.scalar.activation(
                        out=gr[:, col : col + P, :],
                        in_=banks[c][:].rearrange("p t b -> p b t"),
                        func=ACT.Relu,
                    )
            gt[g] = gr

        wbT = const.tile([P, PACK, F, 2], F32)

        def stage_scalars():
            wbps = ps_a.tile([P, 2, PACK, P], BF16, name="pa")
            for j, rows in enumerate((w1_sb, b1_sb)):
                for t in range(PACK):
                    nc.tensor.transpose(wbps[:, j, t, :], rows[:].rearrange("f (p t) -> f t p", t=PACK)[:, t, :], ident_bf[:])
            nc.vector.tensor_copy(out=wbT[:], in_=wbps[:].rearrange("p j t f -> p t f j"))

        def stage_a(g):
            a = h_pool.tile([P, GF, B // RS, PACK, RS], BF16, name="a", align_bytes=64)
            for t in range(PACK):
                for fi in range(GF):
                    f = g * GF + fi
                    nc.vector.tensor_scalar(
                        out=a[:, fi, :, t, :],
                        in0=xc[g // XG][:, (g % XG) * GF + fi, :].rearrange("p (c i) -> p c i", i=RS),
                        scalar1=wbT[:, t, f, 0:1],
                        scalar2=wbT[:, t, f, 1:2],
                        op0=ALU.mult,
                        op1=ALU.add,
                    )
            at[g] = a

        def stage_bg(g):
            gr = g_pool.tile([P, GCOLS, PACK], BF16, name="gr", align_bytes=64)
            nc.gpsimd.tensor_scalar(
                out=gr[:, SC:, :].rearrange("p (c i) t -> p c t i", i=RS),
                in0=at[g][:].rearrange("p f c t i -> p (f c) t i")[:, SC // RS :, :, :],
                scalar1=BIG,
                scalar2=0.0,
                op0=ALU.min,
                op1=ALU.max,
            )
            gt[g] = gr

        def stage_b(g):
            cuts = [0, SC] if g < LAST else [0, HF * B, SC]
            for lo, hi in zip(cuts[:-1], cuts[1:]):
                nc.scalar.activation(
                    out=gt[g][:, lo:hi, :].rearrange("p (c i) t -> p c t i", i=RS),
                    in_=at[g][:].rearrange("p f c t i -> p (f c) t i")[:, lo // RS : hi // RS, :, :],
                    func=ACT.Relu,
                )

        def stage_q(g):
            hc = h_pool.tile([P, GF * B], U32, name="hc", align_bytes=64)
            hs = h_pool.tile([P, GF * B], U8, name="hs", align_bytes=64)
            nc.vector.quantize_mx(
                out=hc[:].bitcast(FP8X4),
                scales=hs[:],
                in_=gt[g][:].rearrange("p c t -> p (c t)"),
            )
            hq[g] = (hc, hs)

        def stage_wr(g):
            ch, off = divmod(g * GF, WF)
            wg = wg_pool.tile([P, GF, E, PACK], BF16, name="wg", align_bytes=64)
            raw = wraw[ch][:, off : off + GF, :].rearrange("p f (t e) -> p f t e", t=PACK)
            es = ES if g >= NPE else 0
            if es > 0:
                nc.scalar.copy(
                    out=wg[:, :, :es, :].rearrange("p f (c i) t -> p f c t i", i=RS),
                    in_=raw[:, :, :, :es].rearrange("p f t (c i) -> p f c t i", i=RS),
                )
            nc.vector.tensor_copy(
                out=wg[:, :, es:, :].rearrange("p f (c i) t -> p f c t i", i=RS),
                in_=raw[:, :, :, es:].rearrange("p f t (c i) -> p f c t i", i=RS),
            )
            wgt[g] = wg

        def stage_wq(g):
            wc = wq_pool.tile([P, GW], U32, name="wc", align_bytes=64)
            ws = wq_pool.tile([P, GW], U8, name="ws", align_bytes=64)
            nc.vector.quantize_mx(
                out=wc[:].bitcast(FP8X4),
                scales=ws[:],
                in_=wgt[g][:].rearrange("p f e t -> p (f e t)"),
            )
            wq[g] = (wc, ws)

        def stage_mm(g):
            hc, hs = hq[g]
            wc, ws = wq[g]
            tiles = []
            for c in range(NBC):
                po = ps_o.tile([P, GW], F32, name="po", tag="po")
                for fi in range(GF):
                    hcol = slice(fi * B + c * P, fi * B + (c + 1) * P)
                    wcol = slice(fi * E, (fi + 1) * E)
                    nc.tensor.matmul_mx(
                        out=po[:, wcol],
                        lhsT=hc[:, hcol].bitcast(FP8X4),
                        lhsT_scale=hs[:, hcol],
                        rhs=wc[:, wcol].bitcast(FP8X4),
                        rhs_scale=ws[:, wcol],
                        start=True,
                        stop=True,
                    )
                tiles.append(po)
            ops[g] = tiles

        first_of = {}
        last_of = {}
        g0 = 0
        for n in STORES:
            for g in range(g0, g0 + n):
                first_of[g] = g0
                last_of[g] = g0 + n - 1
            g0 += n
        assert g0 == NG

        def stage_o(g):
            lo, hi = first_of[g], last_of[g]
            if g == lo:
                ot[lo] = o_pool.tile([P, NBC, max(STORES) * GW], F32, name="ot")
            o = ot[lo]
            pos = g - lo
            for c in range(NBC):
                nc.vector.tensor_tensor(
                    out=o[:, c, pos * GW : (pos + 1) * GW],
                    in0=ops[g][c][:],
                    in1=b2bc[:, g * GW : (g + 1) * GW],
                    op=ALU.add,
                )
            if g == hi:
                for c in range(NBC):
                    nc.sync.dma_start(
                        out=out[c * P : (c + 1) * P, lo * GW : (hi + 1) * GW],
                        in_=o[:, c, : (hi - lo + 1) * GW],
                    )

        tail = {}

        def tail_q(h):
            if h == 0:
                tail["hc"] = h_pool.tile([P, GF * B], U32, name="hc", align_bytes=64)
                tail["hs"] = h_pool.tile([P, GF * B], U8, name="hs", align_bytes=64)
            cols = slice(h * HF * B, (h + 1) * HF * B)
            nc.vector.quantize_mx(
                out=tail["hc"][:, cols].bitcast(FP8X4),
                scales=tail["hs"][:, cols],
                in_=gt[LAST][:, cols, :].rearrange("p c t -> p (c t)"),
            )

        def tail_mm(h):
            wc, ws = wq[LAST]
            for c in range(NBC):
                po = ps_o.tile([P, HF * E], F32, name="po", tag="po")
                for k in range(HF):
                    fi = h * HF + k
                    hcol = slice(fi * B + c * P, fi * B + (c + 1) * P)
                    wcol = slice(fi * E, (fi + 1) * E)
                    nc.tensor.matmul_mx(
                        out=po[:, k * E : (k + 1) * E],
                        lhsT=tail["hc"][:, hcol].bitcast(FP8X4),
                        lhsT_scale=tail["hs"][:, hcol],
                        rhs=wc[:, wcol].bitcast(FP8X4),
                        rhs_scale=ws[:, wcol],
                        start=True,
                        stop=True,
                    )
                tail[(h, c)] = po

        def tail_o(h):
            if h == 0:
                tail["o"] = const.tile([P, NBC, GW], F32, name="otail")
            o = tail["o"]
            n = HF * E
            for c in range(NBC):
                nc.vector.tensor_tensor(
                    out=o[:, c, h * n : (h + 1) * n],
                    in0=tail[(h, c)][:],
                    in1=b2bc[:, LAST * GW + h * n : LAST * GW + (h + 1) * n],
                    op=ALU.add,
                )
                nc.sync.dma_start(
                    out=out[c * P : (c + 1) * P, LAST * GW + h * n : LAST * GW + (h + 1) * n],
                    in_=o[:, c, h * n : (h + 1) * n],
                )

        def ok(g):
            return 0 <= g < NG

        for i in range(-2, NG + 1):
            if NPE <= i + 2 < NG:
                stage_a(i + 2)
                stage_bg(i + 2)
            if i == -2:
                stage_pb(0)
            if i == -1:
                stage_scalars()
            if 1 <= i + 1 < NPE:
                stage_pb(i + 1)
            if 0 <= i < LAST:
                stage_q(i)
                stage_mm(i)
            if i == LAST:
                tail_q(0)
                tail_mm(0)
            if 0 <= i - 1 < LAST:
                stage_o(i - 1)
            if i == LAST:
                tail_q(1)
                tail_mm(1)
                tail_o(0)
            if i - 1 == LAST:
                tail_o(1)
            if ok(i + 1):
                if i + 1 >= NPE:
                    stage_b(i + 1)
                stage_wq(i + 1)
            if ok(i + 2):
                stage_wr(i + 2)
            if i >= 1 and i % 2 == 1 and (i + 7) // 2 < NCH:
                load_w((i + 7) // 2)
            if i >= 2 and i % XG == 2 and (i + 10) // XG < NXC:
                load_x((i + 10) // XG)
            if i in (4, 12):
                load_b2(i // 8 + 2)
